import numpy as np
import ml_dtypes

BF16 = ml_dtypes.bfloat16


def bf(x):
    return np.asarray(x, np.float32).astype(BF16)


def f32(x):
    return np.asarray(x, np.float32)


def f64(x):
    return np.asarray(x).astype(np.float64)


def striped(idx):
    return np.tile(idx.reshape(-1, 16).T, (8, 1))


D, S, N = 128, 2048, 256
TEMP = 0.07
LEVELS = np.repeat(np.arange(1.0, 6.0), (36, 33, 28, 19, 12)) / 32.0


def setup_inputs():
    mags = np.stack([np.random.permutation(LEVELS) for _ in range(S)], axis=1)
    signs = np.where(np.random.random((D, S)) < 0.5, -1.0, 1.0)
    idx = np.random.permutation(np.tile(np.arange(S), 2))[:N]
    return {"table": bf(signs * mags), "w": bf(np.random.standard_normal((D, D)) / np.sqrt(D)), "offs": striped(idx)}


def reference(table, w, offs):
    idx = offs[:16].T.reshape(-1)
    q = f64(w).T @ f64(table)[:, idx]
    return f64(table).T @ q / TEMP

@@ -1,0 +1,53 @@
+import concourse.mybir as mybir
+
+D = 128
+S = 2048
+N = 256
+P = 128
+TEMP = 0.07
+
+BLOCKS = S // P
+BLOCKS_PER_BANK = 512 // N
+BANKS = BLOCKS // BLOCKS_PER_BANK
+
+FLOPS = 2 * D * D * N + 2 * S * D * N
+
+BF16, F32, U16 = mybir.dt.bfloat16, mybir.dt.float32, mybir.dt.uint16
+COPY = mybir.ActivationFunctionType.Copy
+
+
+def tile_cpcloss_kernel(tc, table, w, offs, out):
+    nc = tc.nc
+    out_blocks = out.rearrange("(b p) j -> p b j", p=P)
+
+    with (
+        tc.tile_pool(name="held", bufs=1) as held,
+        tc.tile_pool(name="staging", bufs=BANKS) as staging,
+        tc.psum_pool(name="q_bank", bufs=1) as q_bank,
+        tc.psum_pool(name="score_banks", bufs=4) as score_banks,
+    ):
+        offsets = held.tile([P, N // 16], U16, name="offsets")
+        nc.sync.dma_start(offsets[:], offs)
+        pool_of_steps = held.tile([D, S], BF16, name="pool_of_steps")
+        nc.sync.dma_start(pool_of_steps[:], table)
+        weights = held.tile([D, D], BF16, name="weights")
+        nc.scalar.dma_start(weights[:], w)
+
+        q_f32 = q_bank.tile([D, N], F32, name="q_f32")
+        nc.tensor.matmul(q_f32[:], weights[:], pool_of_steps[:].indirect(offsets[:]), start=True, stop=True)
+        q = held.tile([D, N], BF16, name="q")
+        nc.vector.tensor_copy(q[:], q_f32[:])
+
+        for bank in range(BANKS):
+            first = bank * BLOCKS_PER_BANK
+            scores = score_banks.tile([P, BLOCKS_PER_BANK, N], F32, name="scores")
+            for k in range(BLOCKS_PER_BANK):
+                anchors = pool_of_steps[:, (first + k) * P : (first + k + 1) * P]
+                nc.tensor.matmul(scores[:, k, :], anchors, q[:], start=True, stop=True)
+
+            scaled = staging.tile([P, BLOCKS_PER_BANK, N], F32, name="scaled")
+            if bank % 2 == 0:
+                nc.vector.tensor_scalar_mul(scaled[:], scores[:], 1.0 / TEMP)
+            else:
+                nc.scalar.activation(scaled[:], scores[:], COPY, scale=1.0 / TEMP)
+            nc.sync.dma_start(out_blocks[:, first : first + BLOCKS_PER_BANK, :], scaled[:])

@@ -18,7 +18,7 @@ COPY = mybir.ActivationFunctionType.Copy
 
 def tile_cpcloss_kernel(tc, table, w, offs, out):
     nc = tc.nc
-    out_blocks = out.rearrange("(b p) j -> p b j", p=P)
+    out_blocks = out.rearrange("(p b) j -> p b j", b=BLOCKS)
 
     with (
         tc.tile_pool(name="held", bufs=1) as held,
@@ -38,12 +38,12 @@ def tile_cpcloss_kernel(tc, table, w, offs, out):
         q = held.tile([D, N], BF16, name="q")
         nc.vector.tensor_copy(q[:], q_f32[:])
 
+        anchor_blocks = pool_of_steps[:].rearrange("d (p b) -> d b p", b=BLOCKS)
         for bank in range(BANKS):
             first = bank * BLOCKS_PER_BANK
             scores = score_banks.tile([P, BLOCKS_PER_BANK, N], F32, name="scores")
             for k in range(BLOCKS_PER_BANK):
-                anchors = pool_of_steps[:, (first + k) * P : (first + k + 1) * P]
-                nc.tensor.matmul(scores[:, k, :], anchors, q[:], start=True, stop=True)
+                nc.tensor.matmul(scores[:, k, :], anchor_blocks[:, first + k, :], q[:], start=True, stop=True)
 
             scaled = staging.tile([P, BLOCKS_PER_BANK, N], F32, name="scaled")
             if bank % 2 == 0:

@@ -7,8 +7,8 @@ P = 128
 TEMP = 0.07
 
 BLOCKS = S // P
-BLOCKS_PER_BANK = 512 // N
-BANKS = BLOCKS // BLOCKS_PER_BANK
+LONGEST_STORE = 4
+PSUM_BANKS = 8
 
 FLOPS = 2 * D * D * N + 2 * S * D * N
 
@@ -22,9 +22,9 @@ def tile_cpcloss_kernel(tc, table, w, offs, out):
 
     with (
         tc.tile_pool(name="held", bufs=1) as held,
-        tc.tile_pool(name="staging", bufs=BANKS) as staging,
+        tc.tile_pool(name="staging", bufs=6) as staging,
         tc.psum_pool(name="q_bank", bufs=1) as q_bank,
-        tc.psum_pool(name="score_banks", bufs=4) as score_banks,
+        tc.psum_pool(name="score_banks", bufs=PSUM_BANKS - 1) as score_banks,
     ):
         offsets = held.tile([P, N // 16], U16, name="offsets")
         nc.sync.dma_start(offsets[:], offs)
@@ -39,15 +39,17 @@ def tile_cpcloss_kernel(tc, table, w, offs, out):
         nc.vector.tensor_copy(q[:], q_f32[:])
 
         anchor_blocks = pool_of_steps[:].rearrange("d (p b) -> d b p", b=BLOCKS)
-        for bank in range(BANKS):
-            first = bank * BLOCKS_PER_BANK
-            scores = score_banks.tile([P, BLOCKS_PER_BANK, N], F32, name="scores")
-            for k in range(BLOCKS_PER_BANK):
-                nc.tensor.matmul(scores[:, k, :], anchor_blocks[:, first + k, :], q[:], start=True, stop=True)
-
-            scaled = staging.tile([P, BLOCKS_PER_BANK, N], F32, name="scaled")
-            if bank % 2 == 0:
-                nc.vector.tensor_scalar_mul(scaled[:], scores[:], 1.0 / TEMP)
-            else:
-                nc.scalar.activation(scaled[:], scores[:], COPY, scale=1.0 / TEMP)
-            nc.sync.dma_start(out_blocks[:, first : first + BLOCKS_PER_BANK, :], scaled[:])
+        first = 0
+        while first < BLOCKS:
+            count = min(max(first, 1), LONGEST_STORE)
+            scaled = staging.tile([P, count, N], F32, name="scaled")
+            for k in range(count):
+                block = first + k
+                scores = score_banks.tile([P, N], F32, name="scores")
+                nc.tensor.matmul(scores[:], anchor_blocks[:, block, :], q[:], start=True, stop=True)
+                if block % 2 == 0:
+                    nc.vector.tensor_scalar_mul(scaled[:, k, :], scores[:], 1.0 / TEMP)
+                else:
+                    nc.scalar.activation(scaled[:, k, :], scores[:], COPY, scale=1.0 / TEMP)
+            nc.sync.dma_start(out_blocks[:, first : first + count, :], scaled[:])
+            first += count

@@ -9,6 +9,8 @@ TEMP = 0.07
 BLOCKS = S // P
 LONGEST_STORE = 4
 PSUM_BANKS = 8
+BANK_COLUMNS = 512
+WARM_UPS = 5
 
 FLOPS = 2 * D * D * N + 2 * S * D * N
 
@@ -24,7 +26,8 @@ def tile_cpcloss_kernel(tc, table, w, offs, out):
         tc.tile_pool(name="held", bufs=1) as held,
         tc.tile_pool(name="staging", bufs=6) as staging,
         tc.psum_pool(name="q_bank", bufs=1) as q_bank,
-        tc.psum_pool(name="score_banks", bufs=PSUM_BANKS - 1) as score_banks,
+        tc.psum_pool(name="warm_bank", bufs=1) as warm_bank,
+        tc.psum_pool(name="score_banks", bufs=PSUM_BANKS - 2) as score_banks,
     ):
         offsets = held.tile([P, N // 16], U16, name="offsets")
         nc.sync.dma_start(offsets[:], offs)
@@ -32,6 +35,12 @@ def tile_cpcloss_kernel(tc, table, w, offs, out):
         nc.sync.dma_start(pool_of_steps[:], table)
         weights = held.tile([D, D], BF16, name="weights")
         nc.scalar.dma_start(weights[:], w)
+
+        zeros = held.tile([P, BANK_COLUMNS], BF16, name="zeros")
+        nc.vector.memset(zeros[:], 0.0)
+        unread = warm_bank.tile([P, BANK_COLUMNS], F32, name="unread")
+        for warm_up in range(WARM_UPS):
+            nc.tensor.matmul(unread[:], zeros[:, :P], zeros[:], start=True, stop=True)
 
         q_f32 = q_bank.tile([D, N], F32, name="q_f32")
         nc.tensor.matmul(q_f32[:], weights[:], pool_of_steps[:].indirect(offsets[:]), start=True, stop=True)

@@ -10,7 +10,7 @@ BLOCKS = S // P
 LONGEST_STORE = 4
 PSUM_BANKS = 8
 BANK_COLUMNS = 512
-WARM_UPS = 5
+WARM_UPS = 4
 
 FLOPS = 2 * D * D * N + 2 * S * D * N
 

@@ -7,6 +7,7 @@ P = 128
 TEMP = 0.07
 
 BLOCKS = S // P
+HALF = N // 2
 LONGEST_STORE = 4
 PSUM_BANKS = 8
 BANK_COLUMNS = 512
@@ -22,12 +23,18 @@ def tile_cpcloss_kernel(tc, table, w, offs, out):
     nc = tc.nc
     out_blocks = out.rearrange("(p b) j -> p b j", b=BLOCKS)
 
+    def leave_psum(turn, target, product, factor):
+        if turn % 2 == 0:
+            nc.vector.tensor_scalar_mul(target, product, factor)
+        else:
+            nc.scalar.activation(target, product, COPY, scale=factor)
+
     with (
         tc.tile_pool(name="held", bufs=1) as held,
         tc.tile_pool(name="staging", bufs=6) as staging,
-        tc.psum_pool(name="q_bank", bufs=1) as q_bank,
+        tc.psum_pool(name="q_banks", bufs=2) as q_banks,
         tc.psum_pool(name="warm_bank", bufs=1) as warm_bank,
-        tc.psum_pool(name="score_banks", bufs=PSUM_BANKS - 2) as score_banks,
+        tc.psum_pool(name="score_banks", bufs=PSUM_BANKS - 3) as score_banks,
     ):
         offsets = held.tile([P, N // 16], U16, name="offsets")
         nc.sync.dma_start(offsets[:], offs)
@@ -42,10 +49,14 @@ def tile_cpcloss_kernel(tc, table, w, offs, out):
         for warm_up in range(WARM_UPS):
             nc.tensor.matmul(unread[:], zeros[:, :P], zeros[:], start=True, stop=True)
 
-        q_f32 = q_bank.tile([D, N], F32, name="q_f32")
-        nc.tensor.matmul(q_f32[:], weights[:], pool_of_steps[:].indirect(offsets[:]), start=True, stop=True)
+        halves = [slice(half * HALF, (half + 1) * HALF) for half in range(2)]
+
         q = held.tile([D, N], BF16, name="q")
-        nc.vector.tensor_copy(q[:], q_f32[:])
+        for half, columns in enumerate(halves):
+            q_f32 = q_banks.tile([D, HALF], F32, name="q_f32")
+            looked_up = pool_of_steps[:].indirect(offsets[:, columns.start // 16 : columns.stop // 16])
+            nc.tensor.matmul(q_f32[:], weights[:], looked_up, start=True, stop=True)
+            leave_psum(half, q[:, columns], q_f32[:], 1.0)
 
         anchor_blocks = pool_of_steps[:].rearrange("d (p b) -> d b p", b=BLOCKS)
         first = 0
@@ -54,11 +65,14 @@ def tile_cpcloss_kernel(tc, table, w, offs, out):
             scaled = staging.tile([P, count, N], F32, name="scaled")
             for k in range(count):
                 block = first + k
-                scores = score_banks.tile([P, N], F32, name="scores")
-                nc.tensor.matmul(scores[:], anchor_blocks[:, block, :], q[:], start=True, stop=True)
-                if block % 2 == 0:
-                    nc.vector.tensor_scalar_mul(scaled[:, k, :], scores[:], 1.0 / TEMP)
+                if block == 0:
+                    for half, columns in enumerate(halves):
+                        scores = score_banks.tile([P, N], F32, name="scores")
+                        nc.tensor.matmul(scores[:, columns], anchor_blocks[:, block, :], q[:, columns], start=True, stop=True)
+                        leave_psum(half, scaled[:, k, columns], scores[:, columns], 1.0 / TEMP)
                 else:
-                    nc.scalar.activation(scaled[:, k, :], scores[:], COPY, scale=1.0 / TEMP)
+                    scores = score_banks.tile([P, N], F32, name="scores")
+                    nc.tensor.matmul(scores[:], anchor_blocks[:, block, :], q[:], start=True, stop=True)
+                    leave_psum(block + 1, scaled[:, k, :], scores[:], 1.0 / TEMP)
             nc.sync.dma_start(out_blocks[:, first : first + count, :], scaled[:])
             first += count

@@ -11,7 +11,7 @@ HALF = N // 2
 LONGEST_STORE = 4
 PSUM_BANKS = 8
 BANK_COLUMNS = 512
-WARM_UPS = 4
+WARM_UPS = 6
 
 FLOPS = 2 * D * D * N + 2 * S * D * N
 

@@ -7,7 +7,8 @@ P = 128
 TEMP = 0.07
 
 BLOCKS = S // P
-HALF = N // 2
+PIECES = 4
+PIECE = N // PIECES
 LONGEST_STORE = 4
 PSUM_BANKS = 8
 BANK_COLUMNS = 512
@@ -32,9 +33,8 @@ def tile_cpcloss_kernel(tc, table, w, offs, out):
     with (
         tc.tile_pool(name="held", bufs=1) as held,
         tc.tile_pool(name="staging", bufs=6) as staging,
-        tc.psum_pool(name="q_banks", bufs=2) as q_banks,
         tc.psum_pool(name="warm_bank", bufs=1) as warm_bank,
-        tc.psum_pool(name="score_banks", bufs=PSUM_BANKS - 3) as score_banks,
+        tc.psum_pool(name="banks", bufs=PSUM_BANKS - 1) as banks,
     ):
         offsets = held.tile([P, N // 16], U16, name="offsets")
         nc.sync.dma_start(offsets[:], offs)
@@ -49,14 +49,14 @@ def tile_cpcloss_kernel(tc, table, w, offs, out):
         for warm_up in range(WARM_UPS):
             nc.tensor.matmul(unread[:], zeros[:, :P], zeros[:], start=True, stop=True)
 
-        halves = [slice(half * HALF, (half + 1) * HALF) for half in range(2)]
+        pieces = [slice(piece * PIECE, (piece + 1) * PIECE) for piece in range(PIECES)]
 
         q = held.tile([D, N], BF16, name="q")
-        for half, columns in enumerate(halves):
-            q_f32 = q_banks.tile([D, HALF], F32, name="q_f32")
+        for piece, columns in enumerate(pieces):
+            q_f32 = banks.tile([D, N], F32, name="bank")
             looked_up = pool_of_steps[:].indirect(offsets[:, columns.start // 16 : columns.stop // 16])
-            nc.tensor.matmul(q_f32[:], weights[:], looked_up, start=True, stop=True)
-            leave_psum(half, q[:, columns], q_f32[:], 1.0)
+            nc.tensor.matmul(q_f32[:, columns], weights[:], looked_up, start=True, stop=True)
+            leave_psum(piece, q[:, columns], q_f32[:, columns], 1.0)
 
         anchor_blocks = pool_of_steps[:].rearrange("d (p b) -> d b p", b=BLOCKS)
         first = 0
@@ -66,12 +66,12 @@ def tile_cpcloss_kernel(tc, table, w, offs, out):
             for k in range(count):
                 block = first + k
                 if block == 0:
-                    for half, columns in enumerate(halves):
-                        scores = score_banks.tile([P, N], F32, name="scores")
+                    for piece, columns in enumerate(pieces):
+                        scores = banks.tile([P, N], F32, name="bank")
                         nc.tensor.matmul(scores[:, columns], anchor_blocks[:, block, :], q[:, columns], start=True, stop=True)
-                        leave_psum(half, scaled[:, k, columns], scores[:, columns], 1.0 / TEMP)
+                        leave_psum(piece, scaled[:, k, columns], scores[:, columns], 1.0 / TEMP)
                 else:
-                    scores = score_banks.tile([P, N], F32, name="scores")
+                    scores = banks.tile([P, N], F32, name="bank")
                     nc.tensor.matmul(scores[:], anchor_blocks[:, block, :], q[:], start=True, stop=True)
                     leave_psum(block + 1, scaled[:, k, :], scores[:], 1.0 / TEMP)
             nc.sync.dma_start(out_blocks[:, first : first + count, :], scaled[:])

@@ -36,12 +36,12 @@ def tile_cpcloss_kernel(tc, table, w, offs, out):
         tc.psum_pool(name="warm_bank", bufs=1) as warm_bank,
         tc.psum_pool(name="banks", bufs=PSUM_BANKS - 1) as banks,
     ):
-        offsets = held.tile([P, N // 16], U16, name="offsets")
-        nc.sync.dma_start(offsets[:], offs)
         pool_of_steps = held.tile([D, S], BF16, name="pool_of_steps")
         nc.sync.dma_start(pool_of_steps[:], table)
+        offsets = held.tile([P, N // 16], U16, name="offsets")
+        nc.sync.dma_start(offsets[:], offs)
         weights = held.tile([D, D], BF16, name="weights")
-        nc.scalar.dma_start(weights[:], w)
+        nc.sync.dma_start(weights[:], w)
 
         zeros = held.tile([P, BANK_COLUMNS], BF16, name="zeros")
         nc.vector.memset(zeros[:], 0.0)

@@ -12,7 +12,7 @@ PIECE = N // PIECES
 LONGEST_STORE = 4
 PSUM_BANKS = 8
 BANK_COLUMNS = 512
-WARM_UPS = 6
+WARM_UPS = 5
 
 FLOPS = 2 * D * D * N + 2 * S * D * N
 

@@ -9,7 +9,6 @@ TEMP = 0.07
 BLOCKS = S // P
 PIECES = 4
 PIECE = N // PIECES
-LONGEST_STORE = 4
 PSUM_BANKS = 8
 BANK_COLUMNS = 512
 WARM_UPS = 5
@@ -60,8 +59,11 @@ def tile_cpcloss_kernel(tc, table, w, offs, out):
 
         anchor_blocks = pool_of_steps[:].rearrange("d (p b) -> d b p", b=BLOCKS)
         first = 0
+        count = 0
         while first < BLOCKS:
-            count = min(max(first, 1), LONGEST_STORE)
+            count += 1
+            if BLOCKS - first - count <= count:
+                count = BLOCKS - first
             scaled = staging.tile([P, count, N], F32, name="scaled")
             for k in range(count):
                 block = first + k

@@ -12,6 +12,7 @@ PIECE = N // PIECES
 PSUM_BANKS = 8
 BANK_COLUMNS = 512
 WARM_UPS = 5
+AXI_BURST = 256
 
 FLOPS = 2 * D * D * N + 2 * S * D * N
 
@@ -35,11 +36,11 @@ def tile_cpcloss_kernel(tc, table, w, offs, out):
         tc.psum_pool(name="warm_bank", bufs=1) as warm_bank,
         tc.psum_pool(name="banks", bufs=PSUM_BANKS - 1) as banks,
     ):
-        pool_of_steps = held.tile([D, S], BF16, name="pool_of_steps")
+        pool_of_steps = held.tile([D, S], BF16, name="pool_of_steps", align_bytes=AXI_BURST)
         nc.sync.dma_start(pool_of_steps[:], table)
         offsets = held.tile([P, N // 16], U16, name="offsets")
         nc.sync.dma_start(offsets[:], offs)
-        weights = held.tile([D, D], BF16, name="weights")
+        weights = held.tile([D, D], BF16, name="weights", align_bytes=AXI_BURST)
         nc.sync.dma_start(weights[:], w)
 
         zeros = held.tile([P, BANK_COLUMNS], BF16, name="zeros")
@@ -64,7 +65,7 @@ def tile_cpcloss_kernel(tc, table, w, offs, out):
             count += 1
             if BLOCKS - first - count <= count:
                 count = BLOCKS - first
-            scaled = staging.tile([P, count, N], F32, name="scaled")
+            scaled = staging.tile([P, count, N], F32, name="scaled", align_bytes=AXI_BURST)
             for k in range(count):
                 block = first + k
                 if block == 0:

@@ -12,7 +12,6 @@ PIECE = N // PIECES
 PSUM_BANKS = 8
 BANK_COLUMNS = 512
 WARM_UPS = 5
-AXI_BURST = 256
 
 FLOPS = 2 * D * D * N + 2 * S * D * N
 
@@ -32,15 +31,14 @@ def tile_cpcloss_kernel(tc, table, w, offs, out):
 
     with (
         tc.tile_pool(name="held", bufs=1) as held,
-        tc.tile_pool(name="staging", bufs=6) as staging,
         tc.psum_pool(name="warm_bank", bufs=1) as warm_bank,
         tc.psum_pool(name="banks", bufs=PSUM_BANKS - 1) as banks,
     ):
-        pool_of_steps = held.tile([D, S], BF16, name="pool_of_steps", align_bytes=AXI_BURST)
+        pool_of_steps = held.tile([D, S], BF16, name="pool_of_steps", align_bytes=S * 2)
         nc.sync.dma_start(pool_of_steps[:], table)
         offsets = held.tile([P, N // 16], U16, name="offsets")
         nc.sync.dma_start(offsets[:], offs)
-        weights = held.tile([D, D], BF16, name="weights", align_bytes=AXI_BURST)
+        weights = held.tile([D, D], BF16, name="weights", align_bytes=D * 2)
         nc.sync.dma_start(weights[:], w)
 
         zeros = held.tile([P, BANK_COLUMNS], BF16, name="zeros")
@@ -59,23 +57,22 @@ def tile_cpcloss_kernel(tc, table, w, offs, out):
             leave_psum(piece, q[:, columns], q_f32[:, columns], 1.0)
 
         anchor_blocks = pool_of_steps[:].rearrange("d (p b) -> d b p", b=BLOCKS)
+        scaled = held.tile([P, BLOCKS, N], F32, name="scaled", align_bytes=BLOCKS * N * 4)
         first = 0
         count = 0
         while first < BLOCKS:
             count += 1
             if BLOCKS - first - count <= count:
                 count = BLOCKS - first
-            scaled = staging.tile([P, count, N], F32, name="scaled", align_bytes=AXI_BURST)
-            for k in range(count):
-                block = first + k
+            for block in range(first, first + count):
                 if block == 0:
                     for piece, columns in enumerate(pieces):
                         scores = banks.tile([P, N], F32, name="bank")
                         nc.tensor.matmul(scores[:, columns], anchor_blocks[:, block, :], q[:, columns], start=True, stop=True)
-                        leave_psum(piece, scaled[:, k, columns], scores[:, columns], 1.0 / TEMP)
+                        leave_psum(piece, scaled[:, block, columns], scores[:, columns], 1.0 / TEMP)
                 else:
                     scores = banks.tile([P, N], F32, name="bank")
                     nc.tensor.matmul(scores[:], anchor_blocks[:, block, :], q[:], start=True, stop=True)
-                    leave_psum(block + 1, scaled[:, k, :], scores[:], 1.0 / TEMP)
-            nc.sync.dma_start(out_blocks[:, first : first + count, :], scaled[:])
+                    leave_psum(block + 1, scaled[:, block, :], scores[:], 1.0 / TEMP)
+            nc.sync.dma_start(out_blocks[:, first : first + count, :], scaled[:, first : first + count, :])
             first += count

@@ -9,6 +9,7 @@ TEMP = 0.07
 BLOCKS = S // P
 PIECES = 4
 PIECE = N // PIECES
+HALF = N // 2
 PSUM_BANKS = 8
 BANK_COLUMNS = 512
 WARM_UPS = 5
@@ -58,21 +59,27 @@ def tile_cpcloss_kernel(tc, table, w, offs, out):
 
         anchor_blocks = pool_of_steps[:].rearrange("d (p b) -> d b p", b=BLOCKS)
         scaled = held.tile([P, BLOCKS, N], F32, name="scaled", align_bytes=BLOCKS * N * 4)
+        scores_1 = banks.tile([P, N], F32, name="bank")
+        for piece, columns in enumerate(pieces):
+            scores = banks.tile([P, N], F32, name="bank")
+            nc.tensor.matmul(scores[:, columns], anchor_blocks[:, 0, :], q[:, columns], start=True, stop=True)
+            leave_psum(piece, scaled[:, 0, columns], scores[:, columns], 1.0 / TEMP)
+            if columns.stop % HALF == 0:
+                half = slice(columns.stop - HALF, columns.stop)
+                nc.tensor.matmul(scores_1[:, half], anchor_blocks[:, 1, :], q[:, half], start=True, stop=True)
+
         first = 0
         count = 0
         while first < BLOCKS:
             count += 1
             if BLOCKS - first - count <= count:
                 count = BLOCKS - first
-            for block in range(first, first + count):
-                if block == 0:
-                    for piece, columns in enumerate(pieces):
-                        scores = banks.tile([P, N], F32, name="bank")
-                        nc.tensor.matmul(scores[:, columns], anchor_blocks[:, block, :], q[:, columns], start=True, stop=True)
-                        leave_psum(piece, scaled[:, block, columns], scores[:, columns], 1.0 / TEMP)
+            for block in range(max(first, 1), first + count):
+                if block == 1:
+                    scores = scores_1
                 else:
                     scores = banks.tile([P, N], F32, name="bank")
                     nc.tensor.matmul(scores[:], anchor_blocks[:, block, :], q[:], start=True, stop=True)
-                    leave_psum(block + 1, scaled[:, block, :], scores[:], 1.0 / TEMP)
+                leave_psum(block + 1, scaled[:, block, :], scores[:], 1.0 / TEMP)
             nc.sync.dma_start(out_blocks[:, first : first + count, :], scaled[:, first : first + count, :])
             first += count

import concourse.mybir as mybir

D = 128
S = 2048
N = 256
P = 128
TEMP = 0.07

BLOCKS = S // P
PIECES = 4
PIECE = N // PIECES
HALF = N // 2
PSUM_BANKS = 8
BANK_COLUMNS = 512
WARM_UPS = 5

FLOPS = 2 * D * D * N + 2 * S * D * N

BF16, F32, U16 = mybir.dt.bfloat16, mybir.dt.float32, mybir.dt.uint16
COPY = mybir.ActivationFunctionType.Copy


def tile_cpcloss_kernel(tc, table, w, offs, out):
    nc = tc.nc
    out_blocks = out.rearrange("(p b) j -> p b j", b=BLOCKS)

    def leave_psum(turn, target, product, factor):
        if turn % 2 == 0:
            nc.vector.tensor_scalar_mul(target, product, factor)
        else:
            nc.scalar.activation(target, product, COPY, scale=factor)

    with (
        tc.tile_pool(name="held", bufs=1) as held,
        tc.psum_pool(name="warm_bank", bufs=1) as warm_bank,
        tc.psum_pool(name="banks", bufs=PSUM_BANKS - 1) as banks,
    ):
        pool_of_steps = held.tile([D, S], BF16, name="pool_of_steps", align_bytes=S * 2)
        nc.sync.dma_start(pool_of_steps[:], table)
        offsets = held.tile([P, N // 16], U16, name="offsets")
        nc.sync.dma_start(offsets[:], offs)
        weights = held.tile([D, D], BF16, name="weights", align_bytes=D * 2)
        nc.sync.dma_start(weights[:], w)

        zeros = held.tile([P, BANK_COLUMNS], BF16, name="zeros")
        nc.vector.memset(zeros[:], 0.0)
        unread = warm_bank.tile([P, BANK_COLUMNS], F32, name="unread")
        for warm_up in range(WARM_UPS):
            nc.tensor.matmul(unread[:], zeros[:, :P], zeros[:], start=True, stop=True)

        pieces = [slice(piece * PIECE, (piece + 1) * PIECE) for piece in range(PIECES)]

        q = held.tile([D, N], BF16, name="q")
        for piece, columns in enumerate(pieces):
            q_f32 = banks.tile([D, N], F32, name="bank")
            looked_up = pool_of_steps[:].indirect(offsets[:, columns.start // 16 : columns.stop // 16])
            nc.tensor.matmul(q_f32[:, columns], weights[:], looked_up, start=True, stop=True)
            leave_psum(piece, q[:, columns], q_f32[:, columns], 1.0)

        anchor_blocks = pool_of_steps[:].rearrange("d (p b) -> d b p", b=BLOCKS)
        scaled = held.tile([P, BLOCKS, N], F32, name="scaled", align_bytes=BLOCKS * N * 4)
        scores_1 = banks.tile([P, N], F32, name="bank")
        for piece, columns in enumerate(pieces):
            scores = banks.tile([P, N], F32, name="bank")
            nc.tensor.matmul(scores[:, columns], anchor_blocks[:, 0, :], q[:, columns], start=True, stop=True)
            leave_psum(piece, scaled[:, 0, columns], scores[:, columns], 1.0 / TEMP)
            if columns.stop % HALF == 0:
                half = slice(columns.stop - HALF, columns.stop)
                nc.tensor.matmul(scores_1[:, half], anchor_blocks[:, 1, :], q[:, half], start=True, stop=True)

        first = 0
        count = 0
        while first < BLOCKS:
            count += 1
            if BLOCKS - first - count <= count:
                count = BLOCKS - first
            for block in range(max(first, 1), first + count):
                if block == 1:
                    scores = scores_1
                else:
                    scores = banks.tile([P, N], F32, name="bank")
                    nc.tensor.matmul(scores[:], anchor_blocks[:, block, :], q[:], start=True, stop=True)
                leave_psum(block + 1, scaled[:, block, :], scores[:], 1.0 / TEMP)
            nc.sync.dma_start(out_blocks[:, first : first + count, :], scaled[:, first : first + count, :])
            first += count
